import numpy as np
import ml_dtypes


def mxq(x, axis, fmt="e4m3"):
    dtype, down = {"e4m3": (ml_dtypes.float8_e4m3fn, 7), "e5m2": (ml_dtypes.float8_e5m2, 14)}[fmt]
    v = np.moveaxis(np.asarray(x, np.float32).astype(ml_dtypes.bfloat16).astype(np.float64), axis, -1)
    blocks = v.reshape(v.shape[:-1] + (-1, 32))
    amax = np.abs(blocks).max(-1, keepdims=True)
    byte = np.maximum(np.where(amax > 0, np.frexp(amax)[1] - 1 + 127, 0) - down, 1)
    scale = np.exp2(byte - 127.0)
    codes = (blocks / scale).astype(np.float32).astype(dtype).astype(np.float64)
    return np.moveaxis((codes * scale).reshape(v.shape), -1, axis)


WIDE = False


def mx_kscale(k):
    if not WIDE:
        return np.ones(k)
    levels = np.array([10, -10, 5, -5, 0])
    if k % 512:
        return np.exp2(np.random.permutation(np.resize(levels, k // 32))).repeat(32)
    a = np.empty((k // 512, 16))
    for p in range(k // 512):
        a[p, :8] = np.random.permutation(np.resize(levels, 8))
        for g in range(8):
            far = levels[np.abs(levels - a[p, g]) >= 10]
            a[p, g + 8] = far[np.random.randint(len(far))]
    return np.exp2(a.ravel()).repeat(32)


BF16 = ml_dtypes.bfloat16


def bf(x):
    return np.asarray(x, np.float32).astype(BF16)


def f64(x):
    return np.asarray(x).astype(np.float64)


G, GI, GO, B = 32, 32, 32, 4096
K = G * GI
N = G * GO


def block_gain():
    gain = np.ones((N, K))
    for g in range(G):
        gain[g * GO:(g + 1) * GO, g * GI:(g + 1) * GI] = 0.5
    return gain


def draw0():
    s = mx_kscale(K)
    bound = 1.0 / np.sqrt(K)
    W = np.random.uniform(-bound, bound, (N, K)) * block_gain()
    return {"data": bf(np.random.standard_normal((B, K)) * s),
            "W": bf(W / s[None, :]),
            "b": bf(np.random.standard_normal(N) * 0.3)}


def core(data, W, b):
    return (mxq(f64(data), 1, "e4m3") @ mxq(f64(W), 1, "e4m3").T) + f64(b)


def e4m3fn_bytes(y):
    return np.clip(np.asarray(y, np.float64), -448.0, 448.0).astype(np.float32).astype(ml_dtypes.float8_e4m3fn).view(np.uint8)


def e4m3fn_values(b):
    return np.asarray(b, np.uint8).view(ml_dtypes.float8_e4m3fn).astype(np.float64)


def setup_inputs():
    d = draw0()
    x0 = np.asarray(d['data']).astype(np.float64)
    s = (np.max(np.abs(x0), axis=(0,), keepdims=True) / 448.0).astype(np.float32)
    out = {}
    for k, v in d.items():
        if k == 'data':
            out['data_bytes'] = e4m3fn_bytes(x0 / s.astype(np.float64))
            out['data_scale'] = s
        else:
            out[k] = v
    return out


def reference(data_bytes, data_scale, W, b):
    return core(e4m3fn_values(data_bytes) * data_scale.astype(np.float64), W, b)

@@ -1,0 +1,278 @@
+from contextlib import ExitStack
+
+import concourse.mybir as mybir
+from concourse.masks import make_identity
+
+TOK, K, N = 4096, 1024, 1024
+FLOPS = 2 * TOK * K * N
+
+F32 = mybir.dt.float32
+BF16 = mybir.dt.bfloat16
+U32 = mybir.dt.uint32
+U8 = mybir.dt.uint8
+FP8 = mybir.dt.float8_e4m3fn
+FP8X4 = mybir.dt.float8_e4m3fn_x4
+MULT = mybir.AluOpType.mult
+ADD = mybir.AluOpType.add
+IDENT = mybir.ActivationFunctionType.Identity
+
+P = 128
+NS = 8
+NA = 4
+NG = 2
+LOOK = 3
+NHYB = 6
+ALL_BANKS = ((0, 0), (0, 1), (1, 0), (1, 1))
+
+
+def tile_groupfc_kernel(tc, data_bytes, data_scale, W, b, out):
+    nc = tc.nc
+    with ExitStack() as ctx:
+        const = ctx.enter_context(tc.tile_pool(name="const", bufs=1))
+        xb_pool = ctx.enter_context(tc.tile_pool(name="xbp", bufs=3))
+        xp_pool = ctx.enter_context(tc.tile_pool(name="xpp", bufs=2))
+        grp_pool = ctx.enter_context(tc.tile_pool(name="grpp", bufs=2))
+        code_pool = ctx.enter_context(tc.tile_pool(name="codep", bufs=2))
+        ot_pool = ctx.enter_context(tc.tile_pool(name="otp", bufs=2))
+        res_pool = ctx.enter_context(tc.tile_pool(name="resp", bufs=8))
+        tr_pool = ctx.enter_context(tc.psum_pool(name="trp", bufs=4))
+        acc_pool = ctx.enter_context(tc.psum_pool(name="accp", bufs=4))
+        ctx.enter_context(tc.manual_schedule())
+
+        ident = const.tile([P, P], F32, name="ident")
+        warm = const.tile([P, 2], F32, name="warm")
+        scale_bc = const.tile([P, K], F32, name="scale_bc")
+        bias_bc = const.tile([P, N], F32, name="bias_bc")
+        srow = const.tile([P, P], F32, name="srow")
+        scol = const.tile([P, 8], F32, name="scol")
+        brow_bf = const.tile([P, P], BF16, name="brow_bf")
+        brow_f = const.tile([P, P], F32, name="brow_f")
+        bias_col = const.tile([P, 8], F32, name="bias_col")
+        xbytes = const.tile([P, NS, NA * K], U8, name="xbytes")
+        w_sb = const.tile([P, 4, 2 * K], BF16, name="w_sb")
+        wgrp = const.tile([P, 2 * NG * 512 * 4], BF16, name="wgrp", align_bytes=64)
+        wcodes = const.tile([P, 2 * NG * 512], U32, name="wcodes", align_bytes=64)
+        wscl = const.tile([P, 2 * NG * 512], U8, name="wscl", align_bytes=64)
+
+        bytes_v = data_bytes.rearrange("(s p a) k -> s p (a k)", p=P, a=NA)
+        out_v = out.rearrange("(s p a) n -> s a p n", p=P, a=NA)
+        w_v = W.rearrange("(j p r) k -> p j (r k)", p=P, r=2)
+
+        nc.gpsimd.memset(srow[:], 0.0)
+        nc.vector.memset(brow_bf[:], 0.0)
+        nc.vector.memset(warm[:, 0:1], 0.0)
+        nc.sync.dma_start(out=srow[0:8, :], in_=data_scale.rearrange("o (c p) -> (o c) p", p=P))
+        nc.sync.dma_start(out=xbytes[:, 0, 0:2 * K], in_=bytes_v[0][:, 0:2 * K])
+        nc.sync.dma_start(out=xbytes[:, 0, 2 * K:4 * K], in_=bytes_v[0][:, 2 * K:4 * K])
+        for j in range(4):
+            nc.sync.dma_start(out=w_sb[:, j, :], in_=w_v[:, j, :])
+        nc.scalar.dma_start(out=brow_bf[0:8, :], in_=b.rearrange("(j p) -> j p", p=P))
+        for s in range(1, NS):
+            nc.sync.dma_start(out=xbytes[:, s, :], in_=bytes_v[s])
+
+        make_identity(nc, ident[:])
+        nc.scalar.copy(out=warm[:, 1:2], in_=warm[:, 0:1])
+
+        w_words = w_sb[:].rearrange("p j k -> p (j k)").bitcast(F32)
+        wgrp_words = wgrp[:].bitcast(F32)
+
+        xb = {}
+        xp = {}
+        grp = {}
+        codes = {}
+        scl = {}
+        acc = {}
+        res = {}
+        ot = {}
+
+        def widen(s, a, k0=0, k1=K):
+            if s not in xb:
+                xb[s] = xb_pool.tile([P, NA * K], BF16, name="xb", tag="xb")
+            nc.vector.tensor_tensor(
+                out=xb[s][:, a * K + k0:a * K + k1],
+                in0=xbytes[:, s, a * K + k0:a * K + k1].bitcast(FP8),
+                in1=scale_bc[:, k0:k1],
+                op=MULT,
+            )
+
+        def permute(s):
+            xp[s] = xp_pool.tile([P, 1024], F32, name="xp", tag="xp")
+            nc.scalar.copy(
+                out=xp[s][:].rearrange("p (q u j) -> p q u j", q=4, u=2),
+                in_=xb[s][:, 0:2 * K].bitcast(F32).rearrange("p (q j u) -> p q u j", q=4, u=2),
+            )
+
+        def turn_bank(words, row0, g, dst_words, sorted_words=None, rows_alternate=False):
+            xt = tr_pool.tile([P, 2, 256], F32, name="xt", tag="tr")
+            for r in range(2):
+                for u in range(2):
+                    if sorted_words is None:
+                        base = (row0 + r) * (K // 2) + 256 * g
+                        src = words[:, base + u:base + 256:2]
+                    else:
+                        base = ((row0 + r) * NG + g) * 256 + 128 * u
+                        src = sorted_words[:, base:base + 128]
+                    nc.tensor.transpose(xt[:, u, 128 * r:128 * r + 128], src, ident[:])
+            if rows_alternate:
+                nc.scalar.copy(
+                    out=dst_words.rearrange("p (q r u) -> p q r u", r=2, u=2),
+                    in_=xt[:].rearrange("p u (r q) -> p q r u", r=2),
+                )
+            else:
+                nc.scalar.copy(out=dst_words.rearrange("p (c u) -> p c u", u=2), in_=xt[:].rearrange("p u c -> p c u"))
+
+        def turn_w(nh, hh):
+            for g in range(NG):
+                o = ((nh * NG + g) * 512 + 256 * hh) * 2
+                turn_bank(w_words, 4 * nh + 2 * hh, g, wgrp_words[:, o:o + 512], rows_alternate=True)
+
+        def quant_w(nh):
+            nc.vector.quantize_mx(
+                out=wcodes[:, nh * 1024:(nh + 1) * 1024].bitcast(FP8X4),
+                scales=wscl[:, nh * 1024:(nh + 1) * 1024],
+                in_=wgrp[:, nh * 4096:(nh + 1) * 4096],
+            )
+
+        def turn_x(s, banks):
+            if s not in grp:
+                grp[s] = grp_pool.tile([P, NG * 512 * 4], BF16, name="grp", tag="grp", align_bytes=64)
+            gw = grp[s][:].bitcast(F32)
+            xw = xb[s][:].bitcast(F32)
+            for hh, g in banks:
+                o = (g * 512 + 256 * hh) * 2
+                turn_bank(xw, 2 * hh, g, gw[:, o:o + 512], xp[s][:] if (hh == 0 and s in xp) else None)
+
+        def quant_x(s):
+            codes[s] = code_pool.tile([P, NG * 512], U32, name="codes", tag="codes", align_bytes=64)
+            scl[s] = code_pool.tile([P, NG * 512], U8, name="scl", tag="scl", align_bytes=64)
+            nc.vector.quantize_mx(out=codes[s][:].bitcast(FP8X4), scales=scl[s][:], in_=grp[s][:])
+
+        def mult_d(s, a, nh):
+            acc[(s, a, nh)] = acc_pool.tile([P, 512], F32, name="acc", tag="acc")
+            for g in range(NG):
+                xc = slice(g * 512 + a * P, g * 512 + (a + 1) * P)
+                wc = slice((nh * NG + g) * 512, (nh * NG + g + 1) * 512)
+                nc.tensor.matmul_mx(
+                    out=acc[(s, a, nh)][:],
+                    lhsT=codes[s][:, xc].bitcast(FP8X4),
+                    lhsT_scale=scl[s][:, xc],
+                    rhs=wcodes[:, wc].bitcast(FP8X4),
+                    rhs_scale=wscl[:, wc],
+                    start=(g == 0),
+                    stop=(g == NG - 1),
+                )
+
+        def mult_t(s, jj):
+            at = acc_pool.tile([P, 512], F32, name="acct", tag="acc")
+            for g in range(NG):
+                xc = slice(g * 512, (g + 1) * 512)
+                wc = slice((NG + g) * 512 + jj * P, (NG + g) * 512 + (jj + 1) * P)
+                nc.tensor.matmul_mx(
+                    out=at[:],
+                    lhsT=wcodes[:, wc].bitcast(FP8X4),
+                    lhsT_scale=wscl[:, wc],
+                    rhs=codes[s][:, xc].bitcast(FP8X4),
+                    rhs_scale=scl[s][:, xc],
+                    start=(g == 0),
+                    stop=(g == NG - 1),
+                )
+            if jj == 0:
+                ot[s] = ot_pool.tile([P, 4, 512], F32, name="ot", tag="ot")
+            nc.scalar.activation(out=ot[s][:, jj, :], in_=at[:], func=IDENT, bias=bias_col[:, 4 + jj:5 + jj], scale=1.0)
+
+        def new_res(s):
+            for a in range(NA):
+                res[(s, a)] = res_pool.tile([P, N], F32, name="res", tag="res")
+
+        def turn_back(s, a):
+            tout = tr_pool.tile([P, 512], F32, name="tout", tag="tr")
+            for jj in range(4):
+                nc.tensor.transpose(tout[:, jj * P:(jj + 1) * P], ot[s][:, jj, a * P:(a + 1) * P], ident[:])
+            nc.scalar.copy(out=res[(s, a)][:, 512:1024], in_=tout[:])
+
+        def finish(s, a, nh):
+            nc.vector.tensor_tensor(
+                out=res[(s, a)][:, nh * 512:(nh + 1) * 512],
+                in0=acc[(s, a, nh)][:],
+                in1=bias_bc[:, nh * 512:(nh + 1) * 512],
+                op=ADD,
+            )
+
+        def store(s, a):
+            nc.sync.dma_start(out=out_v[s, a], in_=res[(s, a)][:])
+
+        def store_half(s, a, nh):
+            nc.sync.dma_start(out=out_v[s, a][:, nh * 512:(nh + 1) * 512], in_=res[(s, a)][:, nh * 512:(nh + 1) * 512])
+
+        def spread(col, dst, h, copy):
+            sp = tr_pool.tile([P, 512], F32, name="sp", tag="tr")
+            for c in range(4):
+                nc.tensor.transpose(sp[:, c * P:(c + 1) * P], col[:, 4 * h + c:4 * h + c + 1].to_broadcast([P, P]), ident[:])
+            copy(out=dst[:, 512 * h:512 * (h + 1)], in_=sp[:])
+
+        st = tr_pool.tile([P, P], F32, name="st", tag="tr")
+        nc.tensor.transpose(st[:], srow[:], ident[:])
+        nc.scalar.copy(out=scol[:], in_=st[:, 0:8])
+        spread(scol, scale_bc, 0, nc.vector.tensor_copy)
+        spread(scol, scale_bc, 1, nc.scalar.copy)
+        for g in range(NG):
+            for a in range(NA):
+                widen(0, a, 512 * g, 512 * (g + 1))
+        turn_w(0, 0)
+        turn_w(0, 1)
+        turn_x(0, ((0, 0), (1, 0)))
+        turn_w(1, 0)
+        turn_x(0, ((0, 1), (1, 1)))
+        turn_w(1, 1)
+        nc.scalar.copy(out=brow_f[:], in_=brow_bf[:])
+        bt = tr_pool.tile([P, P], F32, name="bt", tag="tr")
+        nc.tensor.transpose(bt[:], brow_f[:], ident[:])
+        nc.scalar.copy(out=bias_col[:], in_=bt[:, 0:8])
+        spread(bias_col, bias_bc, 0, nc.scalar.copy)
+        spread(bias_col, bias_bc, 1, nc.scalar.copy)
+        quant_w(0)
+        widen(1, 0)
+        widen(1, 1)
+        quant_x(0)
+        quant_w(1)
+        widen(1, 2)
+        widen(1, 3)
+        permute(1)
+        for a in range(NA):
+            widen(2, a)
+
+        for s in range(NS):
+            new_res(s)
+            if s < NHYB:
+                for jj in range(4):
+                    mult_t(s, jj)
+                turn_x(s + 1, ALL_BANKS)
+                for a in range(NA):
+                    mult_d(s, a, 0)
+                finish(s, 0, 0)
+                quant_x(s + 1)
+                finish(s, 1, 0)
+                finish(s, 2, 0)
+                finish(s, 3, 0)
+                if s + LOOK < NS:
+                    for a in range(NA):
+                        widen(s + LOOK, a)
+                permute(s + 2)
+                for a in range(NA):
+                    turn_back(s, a)
+                    store(s, a)
+                if s == NHYB - 1:
+                    turn_x(s + 2, ALL_BANKS)
+            else:
+                for a in range(NA):
+                    mult_d(s, a, 0)
+                    mult_d(s, a, 1)
+                for a in range(NA):
+                    for nh in range(2):
+                        finish(s, a, nh)
+                        if s == NS - 1:
+                            store_half(s, a, nh)
+                    if s < NS - 1:
+                        store(s, a)
+                    if a == 0 and s + 1 < NS:
+                        quant_x(s + 1)

@@ -34,9 +34,9 @@ def tile_groupfc_kernel(tc, data_bytes, data_scale, W, b, out):
         grp_pool = ctx.enter_context(tc.tile_pool(name="grpp", bufs=2))
         code_pool = ctx.enter_context(tc.tile_pool(name="codep", bufs=2))
         ot_pool = ctx.enter_context(tc.tile_pool(name="otp", bufs=2))
-        res_pool = ctx.enter_context(tc.tile_pool(name="resp", bufs=8))
-        tr_pool = ctx.enter_context(tc.psum_pool(name="trp", bufs=4))
-        acc_pool = ctx.enter_context(tc.psum_pool(name="accp", bufs=4))
+        res_pool = ctx.enter_context(tc.tile_pool(name="resp", bufs=12))
+        tr_pool = ctx.enter_context(tc.psum_pool(name="psp", bufs=8))
+        acc_pool = tr_pool
         ctx.enter_context(tc.manual_schedule())
 
         ident = const.tile([P, P], F32, name="ident")
@@ -148,7 +148,7 @@ def tile_groupfc_kernel(tc, data_bytes, data_scale, W, b, out):
             nc.vector.quantize_mx(out=codes[s][:].bitcast(FP8X4), scales=scl[s][:], in_=grp[s][:])
 
         def mult_d(s, a, nh):
-            acc[(s, a, nh)] = acc_pool.tile([P, 512], F32, name="acc", tag="acc")
+            acc[(s, a, nh)] = acc_pool.tile([P, 512], F32, name="acc", tag="tr")
             for g in range(NG):
                 xc = slice(g * 512 + a * P, g * 512 + (a + 1) * P)
                 wc = slice((nh * NG + g) * 512, (nh * NG + g + 1) * 512)
@@ -163,7 +163,7 @@ def tile_groupfc_kernel(tc, data_bytes, data_scale, W, b, out):
                 )
 
         def mult_t(s, jj):
-            at = acc_pool.tile([P, 512], F32, name="acct", tag="acc")
+            at = acc_pool.tile([P, 512], F32, name="acct", tag="tr")
             for g in range(NG):
                 xc = slice(g * 512, (g + 1) * 512)
                 wc = slice((NG + g) * 512 + jj * P, (NG + g) * 512 + (jj + 1) * P)
@@ -241,38 +241,57 @@ def tile_groupfc_kernel(tc, data_bytes, data_scale, W, b, out):
         for a in range(NA):
             widen(2, a)
 
-        for s in range(NS):
+        for s in range(NHYB):
             new_res(s)
-            if s < NHYB:
-                for jj in range(4):
-                    mult_t(s, jj)
-                turn_x(s + 1, ALL_BANKS)
+            if s > 0:
                 for a in range(NA):
-                    mult_d(s, a, 0)
-                finish(s, 0, 0)
-                quant_x(s + 1)
-                finish(s, 1, 0)
-                finish(s, 2, 0)
-                finish(s, 3, 0)
-                if s + LOOK < NS:
-                    for a in range(NA):
-                        widen(s + LOOK, a)
+                    mult_d(s - 1, a, 0)
+            for jj in range(4):
+                mult_t(s, jj)
+            if s > 0:
+                for a in range(NA):
+                    finish(s - 1, a, 0)
+            turn_x(s + 1, ALL_BANKS)
+            if s > 0 and s + 2 < NS:
+                for a in range(NA):
+                    widen(s + 2, a)
+            quant_x(s + 1)
+            for a in range(NA):
+                turn_back(s, a)
+            if s > 0:
+                for a in range(NA):
+                    store(s - 1, a)
+            if s + 2 < NS:
                 permute(s + 2)
-                for a in range(NA):
-                    turn_back(s, a)
-                    store(s, a)
-                if s == NHYB - 1:
-                    turn_x(s + 2, ALL_BANKS)
-            else:
-                for a in range(NA):
-                    mult_d(s, a, 0)
-                    mult_d(s, a, 1)
-                for a in range(NA):
-                    for nh in range(2):
-                        finish(s, a, nh)
-                        if s == NS - 1:
-                            store_half(s, a, nh)
-                    if s < NS - 1:
-                        store(s, a)
-                    if a == 0 and s + 1 < NS:
-                        quant_x(s + 1)
+
+        s = NHYB - 1
+        new_res(s + 1)
+        new_res(s + 2)
+        for a in range(NA):
+            mult_d(s, a, 0)
+        for a in range(2):
+            mult_d(s + 1, a, 0)
+            mult_d(s + 1, a, 1)
+        for a in range(NA):
+            finish(s, a, 0)
+            store(s, a)
+        turn_x(s + 2, ALL_BANKS)
+        for a in range(2):
+            finish(s + 1, a, 0)
+            finish(s + 1, a, 1)
+            store(s + 1, a)
+        quant_x(s + 2)
+        for a in range(2, NA):
+            mult_d(s + 1, a, 0)
+            mult_d(s + 1, a, 1)
+        for a in range(2, NA):
+            finish(s + 1, a, 0)
+            finish(s + 1, a, 1)
+            store(s + 1, a)
+        for a in range(NA):
+            mult_d(s + 2, a, 0)
+            mult_d(s + 2, a, 1)
+        for a in range(NA):
+            for nh in range(2):
+                finish(s + 2, a, nh)
+                store_half(s + 2, a, nh)

@@ -204,20 +204,21 @@ def tile_groupfc_kernel(tc, data_bytes, data_scale, W, b, out):
         def store_half(s, a, nh):
             nc.sync.dma_start(out=out_v[s, a][:, nh * 512:(nh + 1) * 512], in_=res[(s, a)][:, nh * 512:(nh + 1) * 512])
 
-        def spread(col, dst, h, copy):
+        def spread(col, dst, c0, c1, copy):
             sp = tr_pool.tile([P, 512], F32, name="sp", tag="tr")
-            for c in range(4):
-                nc.tensor.transpose(sp[:, c * P:(c + 1) * P], col[:, 4 * h + c:4 * h + c + 1].to_broadcast([P, P]), ident[:])
-            copy(out=dst[:, 512 * h:512 * (h + 1)], in_=sp[:])
+            for c in range(c0, c1):
+                nc.tensor.transpose(sp[:, (c - c0) * P:(c - c0 + 1) * P], col[:, c:c + 1].to_broadcast([P, P]), ident[:])
+            copy(out=dst[:, c0 * P:c1 * P], in_=sp[:, 0:(c1 - c0) * P])
 
         st = tr_pool.tile([P, P], F32, name="st", tag="tr")
         nc.tensor.transpose(st[:], srow[:], ident[:])
         nc.scalar.copy(out=scol[:], in_=st[:, 0:8])
-        spread(scol, scale_bc, 0, nc.vector.tensor_copy)
-        spread(scol, scale_bc, 1, nc.scalar.copy)
-        for g in range(NG):
+        spread(scol, scale_bc, 0, 2, nc.vector.tensor_copy)
+        spread(scol, scale_bc, 2, 4, nc.scalar.copy)
+        spread(scol, scale_bc, 4, 8, nc.scalar.copy)
+        for k0, k1 in ((0, 256), (256, 512), (512, 1024)):
             for a in range(NA):
-                widen(0, a, 512 * g, 512 * (g + 1))
+                widen(0, a, k0, k1)
         turn_w(0, 0)
         turn_w(0, 1)
         turn_x(0, ((0, 0), (1, 0)))
@@ -228,8 +229,8 @@ def tile_groupfc_kernel(tc, data_bytes, data_scale, W, b, out):
         bt = tr_pool.tile([P, P], F32, name="bt", tag="tr")
         nc.tensor.transpose(bt[:], brow_f[:], ident[:])
         nc.scalar.copy(out=bias_col[:], in_=bt[:, 0:8])
-        spread(bias_col, bias_bc, 0, nc.scalar.copy)
-        spread(bias_col, bias_bc, 1, nc.scalar.copy)
+        spread(bias_col, bias_bc, 0, 4, nc.scalar.copy)
+        spread(bias_col, bias_bc, 4, 8, nc.scalar.copy)
         quant_w(0)
         widen(1, 0)
         widen(1, 1)

@@ -43,8 +43,8 @@ def tile_groupfc_kernel(tc, data_bytes, data_scale, W, b, out):
         warm = const.tile([P, 2], F32, name="warm")
         scale_bc = const.tile([P, K], F32, name="scale_bc")
         bias_bc = const.tile([P, N], F32, name="bias_bc")
-        srow = const.tile([P, P], F32, name="srow")
-        scol = const.tile([P, 8], F32, name="scol")
+        scol_a = const.tile([P, 2], F32, name="scol_a")
+        scol_b = const.tile([P, 8], F32, name="scol_b")
         brow_bf = const.tile([P, P], BF16, name="brow_bf")
         brow_f = const.tile([P, P], F32, name="brow_f")
         bias_col = const.tile([P, 8], F32, name="bias_col")
@@ -58,11 +58,14 @@ def tile_groupfc_kernel(tc, data_bytes, data_scale, W, b, out):
         out_v = out.rearrange("(s p a) n -> s a p n", p=P, a=NA)
         w_v = W.rearrange("(j p r) k -> p j (r k)", p=P, r=2)
 
-        nc.gpsimd.memset(srow[:], 0.0)
         nc.vector.memset(brow_bf[:], 0.0)
         nc.vector.memset(warm[:, 0:1], 0.0)
-        nc.sync.dma_start(out=srow[0:8, :], in_=data_scale.rearrange("o (c p) -> (o c) p", p=P))
+        scale_cols = data_scale.rearrange("o (c p) -> p (o c)", p=P)
+        with nc.allow_non_contiguous_dma(reason="one scale to a partition: 4-byte pieces"):
+            nc.sync.dma_start(out=scol_a[:], in_=scale_cols[:, 0:2])
         nc.sync.dma_start(out=xbytes[:, 0, 0:2 * K], in_=bytes_v[0][:, 0:2 * K])
+        with nc.allow_non_contiguous_dma(reason="one scale to a partition: 4-byte pieces"):
+            nc.sync.dma_start(out=scol_b[:, 2:8], in_=scale_cols[:, 2:8])
         nc.sync.dma_start(out=xbytes[:, 0, 2 * K:4 * K], in_=bytes_v[0][:, 2 * K:4 * K])
         for j in range(4):
             nc.sync.dma_start(out=w_sb[:, j, :], in_=w_v[:, j, :])
@@ -166,7 +169,7 @@ def tile_groupfc_kernel(tc, data_bytes, data_scale, W, b, out):
             at = acc_pool.tile([P, 512], F32, name="acct", tag="tr")
             for g in range(NG):
                 xc = slice(g * 512, (g + 1) * 512)
-                wc = slice((NG + g) * 512 + jj * P, (NG + g) * 512 + (jj + 1) * P)
+                wc = slice(g * 512 + jj * P, g * 512 + (jj + 1) * P)
                 nc.tensor.matmul_mx(
                     out=at[:],
                     lhsT=wcodes[:, wc].bitcast(FP8X4),
@@ -178,7 +181,7 @@ def tile_groupfc_kernel(tc, data_bytes, data_scale, W, b, out):
                 )
             if jj == 0:
                 ot[s] = ot_pool.tile([P, 4, 512], F32, name="ot", tag="ot")
-            nc.scalar.activation(out=ot[s][:, jj, :], in_=at[:], func=IDENT, bias=bias_col[:, 4 + jj:5 + jj], scale=1.0)
+            nc.scalar.activation(out=ot[s][:, jj, :], in_=at[:], func=IDENT, bias=bias_col[:, jj:jj + 1], scale=1.0)
 
         def new_res(s):
             for a in range(NA):
@@ -188,7 +191,7 @@ def tile_groupfc_kernel(tc, data_bytes, data_scale, W, b, out):
             tout = tr_pool.tile([P, 512], F32, name="tout", tag="tr")
             for jj in range(4):
                 nc.tensor.transpose(tout[:, jj * P:(jj + 1) * P], ot[s][:, jj, a * P:(a + 1) * P], ident[:])
-            nc.scalar.copy(out=res[(s, a)][:, 512:1024], in_=tout[:])
+            nc.scalar.copy(out=res[(s, a)][:, 0:512], in_=tout[:])
 
         def finish(s, a, nh):
             nc.vector.tensor_tensor(
@@ -210,34 +213,31 @@ def tile_groupfc_kernel(tc, data_bytes, data_scale, W, b, out):
                 nc.tensor.transpose(sp[:, (c - c0) * P:(c - c0 + 1) * P], col[:, c:c + 1].to_broadcast([P, P]), ident[:])
             copy(out=dst[:, c0 * P:c1 * P], in_=sp[:, 0:(c1 - c0) * P])
 
-        st = tr_pool.tile([P, P], F32, name="st", tag="tr")
-        nc.tensor.transpose(st[:], srow[:], ident[:])
-        nc.scalar.copy(out=scol[:], in_=st[:, 0:8])
-        spread(scol, scale_bc, 0, 2, nc.vector.tensor_copy)
-        spread(scol, scale_bc, 2, 4, nc.scalar.copy)
-        spread(scol, scale_bc, 4, 8, nc.scalar.copy)
+        spread(scol_a, scale_bc, 0, 2, nc.vector.tensor_copy)
+        spread(scol_b, scale_bc, 2, 4, nc.scalar.copy)
+        spread(scol_b, scale_bc, 4, 8, nc.scalar.copy)
         for k0, k1 in ((0, 256), (256, 512), (512, 1024)):
             for a in range(NA):
                 widen(0, a, k0, k1)
+        nc.scalar.copy(out=brow_f[:], in_=brow_bf[:])
         turn_w(0, 0)
+        bt = tr_pool.tile([P, P], F32, name="bt", tag="tr")
+        nc.tensor.transpose(bt[:], brow_f[:], ident[:])
+        nc.scalar.copy(out=bias_col[:], in_=bt[:, 0:8])
         turn_w(0, 1)
         turn_x(0, ((0, 0), (1, 0)))
         turn_w(1, 0)
         turn_x(0, ((0, 1), (1, 1)))
         turn_w(1, 1)
-        nc.scalar.copy(out=brow_f[:], in_=brow_bf[:])
-        bt = tr_pool.tile([P, P], F32, name="bt", tag="tr")
-        nc.tensor.transpose(bt[:], brow_f[:], ident[:])
-        nc.scalar.copy(out=bias_col[:], in_=bt[:, 0:8])
         spread(bias_col, bias_bc, 0, 4, nc.scalar.copy)
         spread(bias_col, bias_bc, 4, 8, nc.scalar.copy)
         quant_w(0)
         widen(1, 0)
         widen(1, 1)
         quant_x(0)
-        quant_w(1)
         widen(1, 2)
         widen(1, 3)
+        quant_w(1)
         permute(1)
         for a in range(NA):
             widen(2, a)
@@ -246,12 +246,12 @@ def tile_groupfc_kernel(tc, data_bytes, data_scale, W, b, out):
             new_res(s)
             if s > 0:
                 for a in range(NA):
-                    mult_d(s - 1, a, 0)
+                    mult_d(s - 1, a, 1)
             for jj in range(4):
                 mult_t(s, jj)
             if s > 0:
                 for a in range(NA):
-                    finish(s - 1, a, 0)
+                    finish(s - 1, a, 1)
             turn_x(s + 1, ALL_BANKS)
             if s > 0 and s + 2 < NS:
                 for a in range(NA):
@@ -269,12 +269,12 @@ def tile_groupfc_kernel(tc, data_bytes, data_scale, W, b, out):
         new_res(s + 1)
         new_res(s + 2)
         for a in range(NA):
-            mult_d(s, a, 0)
+            mult_d(s, a, 1)
         for a in range(2):
             mult_d(s + 1, a, 0)
             mult_d(s + 1, a, 1)
         for a in range(NA):
-            finish(s, a, 0)
+            finish(s, a, 1)
             store(s, a)
         turn_x(s + 2, ALL_BANKS)
         for a in range(2):

from contextlib import ExitStack

import concourse.mybir as mybir
from concourse.masks import make_identity

TOK, K, N = 4096, 1024, 1024
FLOPS = 2 * TOK * K * N

F32 = mybir.dt.float32
BF16 = mybir.dt.bfloat16
U32 = mybir.dt.uint32
U8 = mybir.dt.uint8
FP8 = mybir.dt.float8_e4m3fn
FP8X4 = mybir.dt.float8_e4m3fn_x4
MULT = mybir.AluOpType.mult
ADD = mybir.AluOpType.add
IDENT = mybir.ActivationFunctionType.Identity

P = 128
NS = 8
NA = 4
NG = 2
LOOK = 3
NHYB = 6
ALL_BANKS = ((0, 0), (0, 1), (1, 0), (1, 1))


def tile_groupfc_kernel(tc, data_bytes, data_scale, W, b, out):
    nc = tc.nc
    with ExitStack() as ctx:
        const = ctx.enter_context(tc.tile_pool(name="const", bufs=1))
        xb_pool = ctx.enter_context(tc.tile_pool(name="xbp", bufs=3))
        xp_pool = ctx.enter_context(tc.tile_pool(name="xpp", bufs=2))
        grp_pool = ctx.enter_context(tc.tile_pool(name="grpp", bufs=2))
        code_pool = ctx.enter_context(tc.tile_pool(name="codep", bufs=2))
        ot_pool = ctx.enter_context(tc.tile_pool(name="otp", bufs=2))
        res_pool = ctx.enter_context(tc.tile_pool(name="resp", bufs=12))
        tr_pool = ctx.enter_context(tc.psum_pool(name="psp", bufs=8))
        acc_pool = tr_pool
        ctx.enter_context(tc.manual_schedule())

        ident = const.tile([P, P], F32, name="ident")
        warm = const.tile([P, 2], F32, name="warm")
        scale_bc = const.tile([P, K], F32, name="scale_bc")
        bias_bc = const.tile([P, N], F32, name="bias_bc")
        scol_a = const.tile([P, 2], F32, name="scol_a")
        scol_b = const.tile([P, 8], F32, name="scol_b")
        brow_bf = const.tile([P, P], BF16, name="brow_bf")
        brow_f = const.tile([P, P], F32, name="brow_f")
        bias_col = const.tile([P, 8], F32, name="bias_col")
        xbytes = const.tile([P, NS, NA * K], U8, name="xbytes")
        w_sb = const.tile([P, 4, 2 * K], BF16, name="w_sb")
        wgrp = const.tile([P, 2 * NG * 512 * 4], BF16, name="wgrp", align_bytes=64)
        wcodes = const.tile([P, 2 * NG * 512], U32, name="wcodes", align_bytes=64)
        wscl = const.tile([P, 2 * NG * 512], U8, name="wscl", align_bytes=64)

        bytes_v = data_bytes.rearrange("(s p a) k -> s p (a k)", p=P, a=NA)
        out_v = out.rearrange("(s p a) n -> s a p n", p=P, a=NA)
        w_v = W.rearrange("(j p r) k -> p j (r k)", p=P, r=2)

        nc.vector.memset(brow_bf[:], 0.0)
        nc.vector.memset(warm[:, 0:1], 0.0)
        scale_cols = data_scale.rearrange("o (c p) -> p (o c)", p=P)
        with nc.allow_non_contiguous_dma(reason="one scale to a partition: 4-byte pieces"):
            nc.sync.dma_start(out=scol_a[:], in_=scale_cols[:, 0:2])
        nc.sync.dma_start(out=xbytes[:, 0, 0:2 * K], in_=bytes_v[0][:, 0:2 * K])
        with nc.allow_non_contiguous_dma(reason="one scale to a partition: 4-byte pieces"):
            nc.sync.dma_start(out=scol_b[:, 2:8], in_=scale_cols[:, 2:8])
        nc.sync.dma_start(out=xbytes[:, 0, 2 * K:4 * K], in_=bytes_v[0][:, 2 * K:4 * K])
        for j in range(4):
            nc.sync.dma_start(out=w_sb[:, j, :], in_=w_v[:, j, :])
        nc.scalar.dma_start(out=brow_bf[0:8, :], in_=b.rearrange("(j p) -> j p", p=P))
        for s in range(1, NS):
            nc.sync.dma_start(out=xbytes[:, s, :], in_=bytes_v[s])

        make_identity(nc, ident[:])
        nc.scalar.copy(out=warm[:, 1:2], in_=warm[:, 0:1])

        w_words = w_sb[:].rearrange("p j k -> p (j k)").bitcast(F32)
        wgrp_words = wgrp[:].bitcast(F32)

        xb = {}
        xp = {}
        grp = {}
        codes = {}
        scl = {}
        acc = {}
        res = {}
        ot = {}

        def widen(s, a, k0=0, k1=K):
            if s not in xb:
                xb[s] = xb_pool.tile([P, NA * K], BF16, name="xb", tag="xb")
            nc.vector.tensor_tensor(
                out=xb[s][:, a * K + k0:a * K + k1],
                in0=xbytes[:, s, a * K + k0:a * K + k1].bitcast(FP8),
                in1=scale_bc[:, k0:k1],
                op=MULT,
            )

        def permute(s):
            xp[s] = xp_pool.tile([P, 1024], F32, name="xp", tag="xp")
            nc.scalar.copy(
                out=xp[s][:].rearrange("p (q u j) -> p q u j", q=4, u=2),
                in_=xb[s][:, 0:2 * K].bitcast(F32).rearrange("p (q j u) -> p q u j", q=4, u=2),
            )

        def turn_bank(words, row0, g, dst_words, sorted_words=None, rows_alternate=False):
            xt = tr_pool.tile([P, 2, 256], F32, name="xt", tag="tr")
            for r in range(2):
                for u in range(2):
                    if sorted_words is None:
                        base = (row0 + r) * (K // 2) + 256 * g
                        src = words[:, base + u:base + 256:2]
                    else:
                        base = ((row0 + r) * NG + g) * 256 + 128 * u
                        src = sorted_words[:, base:base + 128]
                    nc.tensor.transpose(xt[:, u, 128 * r:128 * r + 128], src, ident[:])
            if rows_alternate:
                nc.scalar.copy(
                    out=dst_words.rearrange("p (q r u) -> p q r u", r=2, u=2),
                    in_=xt[:].rearrange("p u (r q) -> p q r u", r=2),
                )
            else:
                nc.scalar.copy(out=dst_words.rearrange("p (c u) -> p c u", u=2), in_=xt[:].rearrange("p u c -> p c u"))

        def turn_w(nh, hh):
            for g in range(NG):
                o = ((nh * NG + g) * 512 + 256 * hh) * 2
                turn_bank(w_words, 4 * nh + 2 * hh, g, wgrp_words[:, o:o + 512], rows_alternate=True)

        def quant_w(nh):
            nc.vector.quantize_mx(
                out=wcodes[:, nh * 1024:(nh + 1) * 1024].bitcast(FP8X4),
                scales=wscl[:, nh * 1024:(nh + 1) * 1024],
                in_=wgrp[:, nh * 4096:(nh + 1) * 4096],
            )

        def turn_x(s, banks):
            if s not in grp:
                grp[s] = grp_pool.tile([P, NG * 512 * 4], BF16, name="grp", tag="grp", align_bytes=64)
            gw = grp[s][:].bitcast(F32)
            xw = xb[s][:].bitcast(F32)
            for hh, g in banks:
                o = (g * 512 + 256 * hh) * 2
                turn_bank(xw, 2 * hh, g, gw[:, o:o + 512], xp[s][:] if (hh == 0 and s in xp) else None)

        def quant_x(s):
            codes[s] = code_pool.tile([P, NG * 512], U32, name="codes", tag="codes", align_bytes=64)
            scl[s] = code_pool.tile([P, NG * 512], U8, name="scl", tag="scl", align_bytes=64)
            nc.vector.quantize_mx(out=codes[s][:].bitcast(FP8X4), scales=scl[s][:], in_=grp[s][:])

        def mult_d(s, a, nh):
            acc[(s, a, nh)] = acc_pool.tile([P, 512], F32, name="acc", tag="tr")
            for g in range(NG):
                xc = slice(g * 512 + a * P, g * 512 + (a + 1) * P)
                wc = slice((nh * NG + g) * 512, (nh * NG + g + 1) * 512)
                nc.tensor.matmul_mx(
                    out=acc[(s, a, nh)][:],
                    lhsT=codes[s][:, xc].bitcast(FP8X4),
                    lhsT_scale=scl[s][:, xc],
                    rhs=wcodes[:, wc].bitcast(FP8X4),
                    rhs_scale=wscl[:, wc],
                    start=(g == 0),
                    stop=(g == NG - 1),
                )

        def mult_t(s, jj):
            at = acc_pool.tile([P, 512], F32, name="acct", tag="tr")
            for g in range(NG):
                xc = slice(g * 512, (g + 1) * 512)
                wc = slice(g * 512 + jj * P, g * 512 + (jj + 1) * P)
                nc.tensor.matmul_mx(
                    out=at[:],
                    lhsT=wcodes[:, wc].bitcast(FP8X4),
                    lhsT_scale=wscl[:, wc],
                    rhs=codes[s][:, xc].bitcast(FP8X4),
                    rhs_scale=scl[s][:, xc],
                    start=(g == 0),
                    stop=(g == NG - 1),
                )
            if jj == 0:
                ot[s] = ot_pool.tile([P, 4, 512], F32, name="ot", tag="ot")
            nc.scalar.activation(out=ot[s][:, jj, :], in_=at[:], func=IDENT, bias=bias_col[:, jj:jj + 1], scale=1.0)

        def new_res(s):
            for a in range(NA):
                res[(s, a)] = res_pool.tile([P, N], F32, name="res", tag="res")

        def turn_back(s, a):
            tout = tr_pool.tile([P, 512], F32, name="tout", tag="tr")
            for jj in range(4):
                nc.tensor.transpose(tout[:, jj * P:(jj + 1) * P], ot[s][:, jj, a * P:(a + 1) * P], ident[:])
            nc.scalar.copy(out=res[(s, a)][:, 0:512], in_=tout[:])

        def finish(s, a, nh):
            nc.vector.tensor_tensor(
                out=res[(s, a)][:, nh * 512:(nh + 1) * 512],
                in0=acc[(s, a, nh)][:],
                in1=bias_bc[:, nh * 512:(nh + 1) * 512],
                op=ADD,
            )

        def store(s, a):
            nc.sync.dma_start(out=out_v[s, a], in_=res[(s, a)][:])

        def store_half(s, a, nh):
            nc.sync.dma_start(out=out_v[s, a][:, nh * 512:(nh + 1) * 512], in_=res[(s, a)][:, nh * 512:(nh + 1) * 512])

        def spread(col, dst, c0, c1, copy):
            sp = tr_pool.tile([P, 512], F32, name="sp", tag="tr")
            for c in range(c0, c1):
                nc.tensor.transpose(sp[:, (c - c0) * P:(c - c0 + 1) * P], col[:, c:c + 1].to_broadcast([P, P]), ident[:])
            copy(out=dst[:, c0 * P:c1 * P], in_=sp[:, 0:(c1 - c0) * P])

        spread(scol_a, scale_bc, 0, 2, nc.vector.tensor_copy)
        spread(scol_b, scale_bc, 2, 4, nc.scalar.copy)
        spread(scol_b, scale_bc, 4, 8, nc.scalar.copy)
        for k0, k1 in ((0, 256), (256, 512), (512, 1024)):
            for a in range(NA):
                widen(0, a, k0, k1)
        nc.scalar.copy(out=brow_f[:], in_=brow_bf[:])
        turn_w(0, 0)
        bt = tr_pool.tile([P, P], F32, name="bt", tag="tr")
        nc.tensor.transpose(bt[:], brow_f[:], ident[:])
        nc.scalar.copy(out=bias_col[:], in_=bt[:, 0:8])
        turn_w(0, 1)
        turn_x(0, ((0, 0), (1, 0)))
        turn_w(1, 0)
        turn_x(0, ((0, 1), (1, 1)))
        turn_w(1, 1)
        spread(bias_col, bias_bc, 0, 4, nc.scalar.copy)
        spread(bias_col, bias_bc, 4, 8, nc.scalar.copy)
        quant_w(0)
        widen(1, 0)
        widen(1, 1)
        quant_x(0)
        widen(1, 2)
        widen(1, 3)
        quant_w(1)
        permute(1)
        for a in range(NA):
            widen(2, a)

        for s in range(NHYB):
            new_res(s)
            if s > 0:
                for a in range(NA):
                    mult_d(s - 1, a, 1)
            for jj in range(4):
                mult_t(s, jj)
            if s > 0:
                for a in range(NA):
                    finish(s - 1, a, 1)
            turn_x(s + 1, ALL_BANKS)
            if s > 0 and s + 2 < NS:
                for a in range(NA):
                    widen(s + 2, a)
            quant_x(s + 1)
            for a in range(NA):
                turn_back(s, a)
            if s > 0:
                for a in range(NA):
                    store(s - 1, a)
            if s + 2 < NS:
                permute(s + 2)

        s = NHYB - 1
        new_res(s + 1)
        new_res(s + 2)
        for a in range(NA):
            mult_d(s, a, 1)
        for a in range(2):
            mult_d(s + 1, a, 0)
            mult_d(s + 1, a, 1)
        for a in range(NA):
            finish(s, a, 1)
            store(s, a)
        turn_x(s + 2, ALL_BANKS)
        for a in range(2):
            finish(s + 1, a, 0)
            finish(s + 1, a, 1)
            store(s + 1, a)
        quant_x(s + 2)
        for a in range(2, NA):
            mult_d(s + 1, a, 0)
            mult_d(s + 1, a, 1)
        for a in range(2, NA):
            finish(s + 1, a, 0)
            finish(s + 1, a, 1)
            store(s + 1, a)
        for a in range(NA):
            mult_d(s + 2, a, 0)
            mult_d(s + 2, a, 1)
        for a in range(NA):
            for nh in range(2):
                finish(s + 2, a, nh)
                store_half(s + 2, a, nh)
